import numpy as np
import ml_dtypes


def mxq(x, axis, fmt="e4m3"):
    dtype, down = {"e4m3": (ml_dtypes.float8_e4m3fn, 7), "e5m2": (ml_dtypes.float8_e5m2, 14)}[fmt]
    v = np.moveaxis(np.asarray(x, np.float32).astype(ml_dtypes.bfloat16).astype(np.float64), axis, -1)
    blocks = v.reshape(v.shape[:-1] + (-1, 32))
    amax = np.abs(blocks).max(-1, keepdims=True)
    byte = np.maximum(np.where(amax > 0, np.frexp(amax)[1] - 1 + 127, 0) - down, 1)
    scale = np.exp2(byte - 127.0)
    codes = (blocks / scale).astype(np.float32).astype(dtype).astype(np.float64)
    return np.moveaxis((codes * scale).reshape(v.shape), -1, axis)


WIDE = False


def mx_kscale(k):
    if not WIDE:
        return np.ones(k)
    levels = np.array([10, -10, 5, -5, 0])
    a = np.random.permutation(np.resize(levels, k // 512 * 4)).reshape(k // 512, 4)
    idx = np.arange(k)
    return np.exp2(a[idx // 512, idx % 128 // 32])


BF16 = ml_dtypes.bfloat16


def bf(x):
    return np.asarray(x, np.float32).astype(BF16)


def f64(x):
    return np.asarray(x).astype(np.float64)


E2M1 = np.array([0.0, 0.5, 1.0, 1.5, 2.0, 3.0, 4.0, 6.0, -0.0, -0.5, -1.0, -1.5, -2.0, -3.0, -4.0, -6.0])


def pack_weight(w, fmt):
    k, n = w.shape
    w = f64(bf(w)).reshape(k // 32, 32, n)
    amax = np.abs(w).max(1)
    if fmt == "e4m3":
        byte = np.frexp(amax)[1] - 1 + 127 - 7
    else:
        mant, ex = np.frexp(amax / 6.0)
        byte = np.where(mant > 0.5, ex, ex - 1) + 127
    byte = np.clip(np.where(amax > 0, byte, 1), 1, 254)
    scaled = (w * np.exp2(127.0 - byte)[:, None, :]).reshape(k, n).astype(np.float32)
    by_word = np.ascontiguousarray(scaled.reshape(k // 512, 128, 4, n).transpose(0, 1, 3, 2))
    if fmt == "e4m3":
        words = by_word.astype(ml_dtypes.float8_e4m3fn).view(np.uint8)
    else:
        c = by_word.astype(ml_dtypes.float4_e2m1fn).view(np.uint8) & 0xF
        words = c[..., 0::2] | (c[..., 1::2] << 4)
    return np.ascontiguousarray(words), np.ascontiguousarray(byte.astype(np.uint8).reshape(k // 512, 16, n))


def unpack_weight(words, scales, fmt):
    g, p, n, _ = words.shape
    if fmt == "e4m3":
        vals = np.ascontiguousarray(words).view(ml_dtypes.float8_e4m3fn).astype(np.float64)
    else:
        nib = np.empty((g, p, n, 4), np.uint8)
        nib[..., 0::2] = words & 0xF
        nib[..., 1::2] = words >> 4
        vals = E2M1[nib]
    vals = vals * np.repeat(np.exp2(scales.astype(np.float64) - 127.0), 8, axis=1)[..., None]
    return vals.transpose(0, 1, 3, 2).reshape(g * 512, n)


B, T, U, D_ENC, D_PRED, D_JOINT, VOCAB = 4, 64, 32, 512, 512, 512, 1024
LOGIT_CLAMP = 15.0
FMT = "e4m3"


def setup_inputs():
    se, sp = mx_kscale(D_ENC), mx_kscale(D_PRED)
    t = mx_kscale(D_JOINT)
    g = t / t.max()
    encoder_out = bf(np.random.standard_normal((B, T, D_ENC)) * se)
    predictor_out = bf(np.random.standard_normal((B, U, D_PRED)) * sp)
    W_enc_words, W_enc_scales = pack_weight(np.random.standard_normal((D_ENC, D_JOINT)) * 0.7 / np.sqrt(D_ENC) / se[:, None] * g, FMT)
    b_enc = bf(np.random.standard_normal(D_JOINT) * 0.2 * g)
    W_pred_words, W_pred_scales = pack_weight(np.random.standard_normal((D_PRED, D_JOINT)) * 0.7 / np.sqrt(D_PRED) / sp[:, None] * g, FMT)
    b_pred = bf(np.random.standard_normal(D_JOINT) * 0.2 * g)
    W_out_words, W_out_scales = pack_weight(np.random.standard_normal((D_JOINT, VOCAB)) * 8.0 / np.sqrt(D_JOINT) / g[:, None], FMT)
    b_out = bf(np.random.standard_normal(VOCAB) * 0.5)
    return {"encoder_out": encoder_out,
            "predictor_out": predictor_out,
            "W_enc_words": W_enc_words,
            "W_enc_scales": W_enc_scales,
            "b_enc": b_enc,
            "W_pred_words": W_pred_words,
            "W_pred_scales": W_pred_scales,
            "b_pred": b_pred,
            "W_out_words": W_out_words,
            "W_out_scales": W_out_scales,
            "b_out": b_out}


def reference(encoder_out, predictor_out, W_enc_words, W_enc_scales, b_enc, W_pred_words, W_pred_scales, b_pred, W_out_words, W_out_scales, b_out):
    enc = (mxq(f64(encoder_out), 2, "e4m3") @ unpack_weight(W_enc_words, W_enc_scales, FMT)) + f64(b_enc)
    pred = (mxq(f64(predictor_out), 2, "e4m3") @ unpack_weight(W_pred_words, W_pred_scales, FMT)) + f64(b_pred)
    joint = np.tanh(enc[:, :, None, :] + pred[:, None, :, :])
    logits = (mxq(joint, 3, "e4m3") @ unpack_weight(W_out_words, W_out_scales, FMT)) + f64(b_out)
    return np.clip(logits, -LOGIT_CLAMP, LOGIT_CLAMP)

@@ -1,0 +1,193 @@
+from contextlib import ExitStack
+
+import concourse.mybir as mybir
+from concourse.masks import make_identity
+
+F32 = mybir.dt.float32
+BF16 = mybir.dt.bfloat16
+I32 = mybir.dt.int32
+U32 = mybir.dt.uint32
+U8 = mybir.dt.uint8
+FP8X4 = mybir.dt.float8_e4m3fn_x4
+TANH = mybir.ActivationFunctionType.Tanh
+ADD = mybir.AluOpType.add
+MIN = mybir.AluOpType.min
+MAX = mybir.AluOpType.max
+
+P = 128
+PACK = 4
+BATCH, T_LEN, U_LEN = 4, 64, 32
+DEPTH = P * PACK
+VOCAB = 1024
+BANK = 512
+CLAMP = 15.0
+U_STEP = 2
+FLOPS = 2 * DEPTH * (BATCH * T_LEN * DEPTH + BATCH * U_LEN * DEPTH + BATCH * T_LEN * U_LEN * VOCAB)
+
+
+def load_weight(nc, keep, words, scales, label):
+    cols = words.shape[2]
+    codes = keep.tile([P, PACK * cols], U8, name=label + "_codes", align_bytes=64)
+    scale_rows = keep.tile([P, cols], U8, name=label + "_scales", align_bytes=64)
+    nc.vector.memset(scale_rows[:].bitcast(I32), 0)
+    nc.sync.dma_start(
+        out=codes[:].bitcast(I32), in_=words[0].rearrange("p n t -> p (n t)").bitcast(I32)
+    )
+    for r in range(4):
+        nc.sync.dma_start(
+            out=scale_rows[r:P:32, :].bitcast(I32), in_=scales[0, r:16:4, :].bitcast(I32)
+        )
+    return codes, scale_rows
+
+
+def tile_jointnetwork_kernel(
+    tc,
+    encoder_out,
+    predictor_out,
+    W_enc_words,
+    W_enc_scales,
+    b_enc,
+    W_pred_words,
+    W_pred_scales,
+    b_pred,
+    W_out_words,
+    W_out_scales,
+    b_out,
+    out,
+):
+    nc = tc.nc
+    with ExitStack() as ctx:
+        keep = ctx.enter_context(tc.tile_pool(name="keep", bufs=1))
+        stage = ctx.enter_context(tc.tile_pool(name="stage", bufs=3))
+        work = ctx.enter_context(tc.tile_pool(name="work", bufs=3))
+        result = ctx.enter_context(tc.tile_pool(name="result", bufs=4))
+        psum = ctx.enter_context(tc.psum_pool(name="psum", bufs=8))
+
+        enc_rows = encoder_out.flatten_outer_dims()
+        x_pred = keep.tile([P, DEPTH], BF16)
+        x_enc0 = keep.tile([P, DEPTH], BF16)
+        x_enc1 = keep.tile([P, DEPTH], BF16)
+        nc.scalar.dma_start(out=x_pred[:], in_=predictor_out.flatten_outer_dims())
+        nc.scalar.dma_start(out=x_enc0[:], in_=enc_rows[0:P, :])
+        w_pred, w_pred_scales = load_weight(nc, keep, W_pred_words, W_pred_scales, "w_pred")
+        w_enc, w_enc_scales = load_weight(nc, keep, W_enc_words, W_enc_scales, "w_enc")
+        b_enc_sb = keep.tile([P, PACK], BF16)
+        b_pred_sb = keep.tile([P, PACK], BF16)
+        nc.scalar.dma_start(out=b_enc_sb[:], in_=b_enc.rearrange("(p j) -> p j", j=PACK))
+        nc.scalar.dma_start(out=b_pred_sb[:], in_=b_pred.rearrange("(p j) -> p j", j=PACK))
+        nc.scalar.dma_start(out=x_enc1[:], in_=enc_rows[P : 2 * P, :])
+        w_out, w_out_scales = load_weight(nc, keep, W_out_words, W_out_scales, "w_out")
+        b_out_sb = keep.tile([P, VOCAB], BF16)
+        nc.scalar.dma_start(out=b_out_sb[:], in_=b_out.partition_broadcast(P))
+
+        identity = keep.tile([P, P], F32)
+        make_identity(nc, identity[:])
+
+        warm = keep.tile([P, 1], F32)
+        nc.vector.memset(warm[:], 0.0)
+        nc.scalar.activation(out=warm[:], in_=warm[:], func=TANH)
+
+        b_sum = keep.tile([P, PACK], F32)
+        nc.vector.tensor_tensor(out=b_sum[:], in0=b_enc_sb[:], in1=b_pred_sb[:], op=ADD)
+
+        def project(x_rows, w_codes, w_scale_rows, copy):
+            x_words = x_rows[:].bitcast(F32)
+            pairs = psum.tile([P, BANK], F32, tag="bank")
+            pairs_view = pairs[:, 0 : 2 * P].rearrange("p (h r) -> p h r", h=2)
+            for h in range(2):
+                nc.tensor.transpose(pairs_view[:, h, :], x_words[:, h : DEPTH // 2 : 2], identity[:])
+            grouped = stage.tile([P, PACK * P], BF16, align_bytes=64)
+            copy(
+                out=grouped[:].bitcast(F32).rearrange("p (r h) -> p r h", h=2),
+                in_=pairs_view.rearrange("p h r -> p r h"),
+            )
+            x_codes = stage.tile([P, P], U32, align_bytes=64)
+            x_scales = stage.tile([P, P], U8, align_bytes=64)
+            nc.vector.quantize_mx(out=x_codes[:].bitcast(FP8X4), scales=x_scales[:], in_=grouped[:])
+            product = psum.tile([P, BANK], F32, tag="bank")
+            nc.tensor.matmul_mx(
+                out=product[:],
+                lhsT=x_codes[:].bitcast(FP8X4),
+                lhsT_scale=x_scales[:],
+                rhs=w_codes[:].bitcast(FP8X4),
+                rhs_scale=w_scale_rows[:],
+                start=True,
+                stop=True,
+            )
+            by_j = stage.tile([P, PACK, P], F32)
+            copy(out=by_j[:], in_=product[:].rearrange("r (p j) -> r j p", j=PACK))
+            turned = psum.tile([P, BANK], F32, tag="bank")
+            turned_view = turned[:].rearrange("p (j r) -> p j r", j=PACK)
+            for j in range(PACK):
+                nc.tensor.transpose(turned_view[:, j, :], by_j[:, j, :], identity[:])
+            return turned_view
+
+        pred_T = keep.tile([P, PACK, P], F32)
+        enc_T = [keep.tile([P, PACK, P], F32, name="enc_T%d" % pair) for pair in range(2)]
+        turned_pred = project(x_pred, w_pred, w_pred_scales, nc.vector.tensor_copy)
+        nc.vector.tensor_tensor(
+            out=pred_T[:],
+            in0=turned_pred,
+            in1=b_sum[:].unsqueeze(2).to_broadcast([P, PACK, P]),
+            op=ADD,
+        )
+        turned_enc0 = project(x_enc0, w_enc, w_enc_scales, nc.scalar.copy)
+        nc.scalar.copy(out=enc_T[0][:], in_=turned_enc0)
+        turned_enc1 = project(x_enc1, w_enc, w_enc_scales, nc.vector.tensor_copy)
+        nc.vector.tensor_copy(out=enc_T[1][:], in_=turned_enc1)
+
+        out_rows = out.rearrange("b t u v -> (b t) u v")
+        for pair in range(BATCH // 2):
+            for u0 in range(0, U_LEN, U_STEP):
+                planes = work.tile([P, PACK, U_STEP, P], BF16)
+                for i in range(U_STEP):
+                    for half in range(2):
+                        rows = slice(half * T_LEN, (half + 1) * T_LEN)
+                        col = (2 * pair + half) * U_LEN + u0 + i
+                        for j in range(PACK):
+                            nc.scalar.activation(
+                                out=planes[:, j, i, rows],
+                                in_=enc_T[pair][:, j, rows],
+                                func=TANH,
+                                bias=pred_T[:, j, col : col + 1],
+                                scale=1.0,
+                            )
+                grouped = work.tile([P, U_STEP * P, PACK], BF16, align_bytes=64)
+                nc.scalar.copy(
+                    out=grouped[:].rearrange("p (c r) j -> p c j r", r=4),
+                    in_=planes[:].rearrange("p j i m -> p j (i m)").rearrange("p j (c r) -> p c j r", r=4),
+                )
+                codes = work.tile([P, U_STEP * P], U32, align_bytes=64)
+                scales = work.tile([P, U_STEP * P], U8, align_bytes=64)
+                nc.vector.quantize_mx(
+                    out=codes[:].bitcast(FP8X4),
+                    scales=scales[:],
+                    in_=grouped[:].rearrange("p c j -> p (c j)"),
+                )
+                logits = result.tile([P, U_STEP, VOCAB], F32)
+                for i in range(U_STEP):
+                    m_cols = slice(i * P, (i + 1) * P)
+                    for v0 in range(0, VOCAB, BANK):
+                        acc = psum.tile([P, BANK], F32, tag="bank")
+                        nc.tensor.matmul_mx(
+                            out=acc[:],
+                            lhsT=codes[:, m_cols].bitcast(FP8X4),
+                            lhsT_scale=scales[:, m_cols],
+                            rhs=w_out[:, PACK * v0 : PACK * (v0 + BANK)].bitcast(FP8X4),
+                            rhs_scale=w_out_scales[:, v0 : v0 + BANK],
+                            start=True,
+                            stop=True,
+                        )
+                        nc.vector.tensor_tensor(
+                            out=logits[:, i, v0 : v0 + BANK],
+                            in0=acc[:],
+                            in1=b_out_sb[:, v0 : v0 + BANK],
+                            op=ADD,
+                        )
+                flat = logits[:].rearrange("p i v -> p (i v)")
+                nc.gpsimd.tensor_scalar(
+                    out=flat, in0=flat, scalar1=CLAMP, scalar2=-CLAMP, op0=MIN, op1=MAX
+                )
+                nc.sync.dma_start(
+                    out=out_rows[pair * P : (pair + 1) * P, u0 : u0 + U_STEP, :], in_=logits[:]
+                )

@@ -62,20 +62,20 @@ def tile_jointnetwork_kernel(
         work = ctx.enter_context(tc.tile_pool(name="work", bufs=3))
         result = ctx.enter_context(tc.tile_pool(name="result", bufs=4))
         psum = ctx.enter_context(tc.psum_pool(name="psum", bufs=8))
+        ctx.enter_context(tc.manual_schedule())
 
         enc_rows = encoder_out.flatten_outer_dims()
         x_pred = keep.tile([P, DEPTH], BF16)
-        x_enc0 = keep.tile([P, DEPTH], BF16)
-        x_enc1 = keep.tile([P, DEPTH], BF16)
+        x_enc = [keep.tile([P, DEPTH], BF16, name="x_enc%d" % pair) for pair in range(2)]
         nc.scalar.dma_start(out=x_pred[:], in_=predictor_out.flatten_outer_dims())
-        nc.scalar.dma_start(out=x_enc0[:], in_=enc_rows[0:P, :])
+        nc.scalar.dma_start(out=x_enc[0][:], in_=enc_rows[0:P, :])
         w_pred, w_pred_scales = load_weight(nc, keep, W_pred_words, W_pred_scales, "w_pred")
         w_enc, w_enc_scales = load_weight(nc, keep, W_enc_words, W_enc_scales, "w_enc")
         b_enc_sb = keep.tile([P, PACK], BF16)
         b_pred_sb = keep.tile([P, PACK], BF16)
         nc.scalar.dma_start(out=b_enc_sb[:], in_=b_enc.rearrange("(p j) -> p j", j=PACK))
         nc.scalar.dma_start(out=b_pred_sb[:], in_=b_pred.rearrange("(p j) -> p j", j=PACK))
-        nc.scalar.dma_start(out=x_enc1[:], in_=enc_rows[P : 2 * P, :])
+        nc.scalar.dma_start(out=x_enc[1][:], in_=enc_rows[P : 2 * P, :])
         w_out, w_out_scales = load_weight(nc, keep, W_out_words, W_out_scales, "w_out")
         b_out_sb = keep.tile([P, VOCAB], BF16)
         nc.scalar.dma_start(out=b_out_sb[:], in_=b_out.partition_broadcast(P))
@@ -87,107 +87,143 @@ def tile_jointnetwork_kernel(
         nc.vector.memset(warm[:], 0.0)
         nc.scalar.activation(out=warm[:], in_=warm[:], func=TANH)
 
-        b_sum = keep.tile([P, PACK], F32)
-        nc.vector.tensor_tensor(out=b_sum[:], in0=b_enc_sb[:], in1=b_pred_sb[:], op=ADD)
-
-        def project(x_rows, w_codes, w_scale_rows, copy):
-            x_words = x_rows[:].bitcast(F32)
-            pairs = psum.tile([P, BANK], F32, tag="bank")
-            pairs_view = pairs[:, 0 : 2 * P].rearrange("p (h r) -> p h r", h=2)
-            for h in range(2):
-                nc.tensor.transpose(pairs_view[:, h, :], x_words[:, h : DEPTH // 2 : 2], identity[:])
-            grouped = stage.tile([P, PACK * P], BF16, align_bytes=64)
-            copy(
-                out=grouped[:].bitcast(F32).rearrange("p (r h) -> p r h", h=2),
-                in_=pairs_view.rearrange("p h r -> p r h"),
-            )
-            x_codes = stage.tile([P, P], U32, align_bytes=64)
-            x_scales = stage.tile([P, P], U8, align_bytes=64)
-            nc.vector.quantize_mx(out=x_codes[:].bitcast(FP8X4), scales=x_scales[:], in_=grouped[:])
-            product = psum.tile([P, BANK], F32, tag="bank")
-            nc.tensor.matmul_mx(
-                out=product[:],
-                lhsT=x_codes[:].bitcast(FP8X4),
-                lhsT_scale=x_scales[:],
-                rhs=w_codes[:].bitcast(FP8X4),
-                rhs_scale=w_scale_rows[:],
-                start=True,
-                stop=True,
-            )
-            by_j = stage.tile([P, PACK, P], F32)
-            copy(out=by_j[:], in_=product[:].rearrange("r (p j) -> r j p", j=PACK))
-            turned = psum.tile([P, BANK], F32, tag="bank")
-            turned_view = turned[:].rearrange("p (j r) -> p j r", j=PACK)
-            for j in range(PACK):
-                nc.tensor.transpose(turned_view[:, j, :], by_j[:, j, :], identity[:])
-            return turned_view
+        def project(jobs):
+            for job in jobs:
+                x_words = job["x"][:].bitcast(F32)
+                pairs = psum.tile([P, BANK], F32, tag="bank")
+                job["pairs"] = pairs[:, 0 : 2 * P].rearrange("p (h r) -> p h r", h=2)
+                for h in range(2):
+                    nc.tensor.transpose(
+                        job["pairs"][:, h, :], x_words[:, h : DEPTH // 2 : 2], identity[:]
+                    )
+            for job in jobs:
+                grouped = stage.tile([P, PACK * P], BF16, align_bytes=64)
+                job["grouped"] = grouped
+                job["copy"](
+                    out=grouped[:].bitcast(F32).rearrange("p (r h) -> p r h", h=2),
+                    in_=job["pairs"].rearrange("p h r -> p r h"),
+                )
+            for job in jobs:
+                x_codes = stage.tile([P, P], U32, align_bytes=64)
+                x_scales = stage.tile([P, P], U8, align_bytes=64)
+                nc.vector.quantize_mx(
+                    out=x_codes[:].bitcast(FP8X4), scales=x_scales[:], in_=job["grouped"][:]
+                )
+                product = psum.tile([P, BANK], F32, tag="bank")
+                job["product"] = product
+                nc.tensor.matmul_mx(
+                    out=product[:],
+                    lhsT=x_codes[:].bitcast(FP8X4),
+                    lhsT_scale=x_scales[:],
+                    rhs=job["w"][:].bitcast(FP8X4),
+                    rhs_scale=job["w_scales"][:],
+                    start=True,
+                    stop=True,
+                )
+            for job in jobs:
+                by_j = stage.tile([P, PACK, P], F32)
+                job["by_j"] = by_j
+                job["copy"](out=by_j[:], in_=job["product"][:].rearrange("r (p j) -> r j p", j=PACK))
+            for job in jobs:
+                turned = psum.tile([P, BANK], F32, tag="bank")
+                job["turned"] = turned[:].rearrange("p (j r) -> p j r", j=PACK)
+                for j in range(PACK):
+                    nc.tensor.transpose(job["turned"][:, j, :], job["by_j"][:, j, :], identity[:])
 
         pred_T = keep.tile([P, PACK, P], F32)
         enc_T = [keep.tile([P, PACK, P], F32, name="enc_T%d" % pair) for pair in range(2)]
-        turned_pred = project(x_pred, w_pred, w_pred_scales, nc.vector.tensor_copy)
+        pred_job = {"x": x_pred, "w": w_pred, "w_scales": w_pred_scales, "copy": nc.vector.tensor_copy}
+        enc_jobs = [
+            {"x": x_enc[0], "w": w_enc, "w_scales": w_enc_scales, "copy": nc.scalar.copy},
+            {"x": x_enc[1], "w": w_enc, "w_scales": w_enc_scales, "copy": nc.vector.tensor_copy},
+        ]
+        project([pred_job, enc_jobs[0]])
+        b_sum = keep.tile([P, PACK], F32)
+        nc.vector.tensor_tensor(out=b_sum[:], in0=b_enc_sb[:], in1=b_pred_sb[:], op=ADD)
         nc.vector.tensor_tensor(
             out=pred_T[:],
-            in0=turned_pred,
+            in0=pred_job["turned"],
             in1=b_sum[:].unsqueeze(2).to_broadcast([P, PACK, P]),
             op=ADD,
         )
-        turned_enc0 = project(x_enc0, w_enc, w_enc_scales, nc.scalar.copy)
-        nc.scalar.copy(out=enc_T[0][:], in_=turned_enc0)
-        turned_enc1 = project(x_enc1, w_enc, w_enc_scales, nc.vector.tensor_copy)
-        nc.vector.tensor_copy(out=enc_T[1][:], in_=turned_enc1)
+        nc.scalar.copy(out=enc_T[0][:], in_=enc_jobs[0]["turned"])
 
         out_rows = out.rearrange("b t u v -> (b t) u v")
-        for pair in range(BATCH // 2):
-            for u0 in range(0, U_LEN, U_STEP):
-                planes = work.tile([P, PACK, U_STEP, P], BF16)
-                for i in range(U_STEP):
-                    for half in range(2):
-                        rows = slice(half * T_LEN, (half + 1) * T_LEN)
-                        col = (2 * pair + half) * U_LEN + u0 + i
-                        for j in range(PACK):
-                            nc.scalar.activation(
-                                out=planes[:, j, i, rows],
-                                in_=enc_T[pair][:, j, rows],
-                                func=TANH,
-                                bias=pred_T[:, j, col : col + 1],
-                                scale=1.0,
-                            )
-                grouped = work.tile([P, U_STEP * P, PACK], BF16, align_bytes=64)
-                nc.scalar.copy(
-                    out=grouped[:].rearrange("p (c r) j -> p c j r", r=4),
-                    in_=planes[:].rearrange("p j i m -> p j (i m)").rearrange("p j (c r) -> p c j r", r=4),
-                )
-                codes = work.tile([P, U_STEP * P], U32, align_bytes=64)
-                scales = work.tile([P, U_STEP * P], U8, align_bytes=64)
-                nc.vector.quantize_mx(
-                    out=codes[:].bitcast(FP8X4),
-                    scales=scales[:],
-                    in_=grouped[:].rearrange("p c j -> p (c j)"),
-                )
-                logits = result.tile([P, U_STEP, VOCAB], F32)
-                for i in range(U_STEP):
-                    m_cols = slice(i * P, (i + 1) * P)
-                    for v0 in range(0, VOCAB, BANK):
-                        acc = psum.tile([P, BANK], F32, tag="bank")
-                        nc.tensor.matmul_mx(
-                            out=acc[:],
-                            lhsT=codes[:, m_cols].bitcast(FP8X4),
-                            lhsT_scale=scales[:, m_cols],
-                            rhs=w_out[:, PACK * v0 : PACK * (v0 + BANK)].bitcast(FP8X4),
-                            rhs_scale=w_out_scales[:, v0 : v0 + BANK],
-                            start=True,
-                            stop=True,
+        rounds = [(pair, u0) for pair in range(BATCH // 2) for u0 in range(0, U_LEN, U_STEP)]
+
+        def joint_round(pair, u0):
+            planes = work.tile([P, PACK, U_STEP, P], BF16)
+            for i in range(U_STEP):
+                for half in range(2):
+                    rows = slice(half * T_LEN, (half + 1) * T_LEN)
+                    col = (2 * pair + half) * U_LEN + u0 + i
+                    for j in range(PACK):
+                        nc.scalar.activation(
+                            out=planes[:, j, i, rows],
+                            in_=enc_T[pair][:, j, rows],
+                            func=TANH,
+                            bias=pred_T[:, j, col : col + 1],
+                            scale=1.0,
                         )
-                        nc.vector.tensor_tensor(
-                            out=logits[:, i, v0 : v0 + BANK],
-                            in0=acc[:],
-                            in1=b_out_sb[:, v0 : v0 + BANK],
-                            op=ADD,
-                        )
-                flat = logits[:].rearrange("p i v -> p (i v)")
-                nc.gpsimd.tensor_scalar(
-                    out=flat, in0=flat, scalar1=CLAMP, scalar2=-CLAMP, op0=MIN, op1=MAX
+            grouped = work.tile([P, U_STEP * P, PACK], BF16, align_bytes=64)
+            nc.scalar.copy(
+                out=grouped[:].rearrange("p (c r) j -> p c j r", r=4),
+                in_=planes[:].rearrange("p j i m -> p j (i m)").rearrange("p j (c r) -> p c j r", r=4),
+            )
+            return grouped
+
+        def multiply_round(grouped):
+            codes = work.tile([P, U_STEP * P], U32, align_bytes=64)
+            scales = work.tile([P, U_STEP * P], U8, align_bytes=64)
+            nc.vector.quantize_mx(
+                out=codes[:].bitcast(FP8X4),
+                scales=scales[:],
+                in_=grouped[:].rearrange("p c j -> p (c j)"),
+            )
+            banks = []
+            for i in range(U_STEP):
+                m_cols = slice(i * P, (i + 1) * P)
+                for v0 in range(0, VOCAB, BANK):
+                    acc = psum.tile([P, BANK], F32, tag="bank")
+                    nc.tensor.matmul_mx(
+                        out=acc[:],
+                        lhsT=codes[:, m_cols].bitcast(FP8X4),
+                        lhsT_scale=scales[:, m_cols],
+                        rhs=w_out[:, PACK * v0 : PACK * (v0 + BANK)].bitcast(FP8X4),
+                        rhs_scale=w_out_scales[:, v0 : v0 + BANK],
+                        start=True,
+                        stop=True,
+                    )
+                    banks.append((i, v0, acc))
+            return banks
+
+        def finish_round(pair, u0, banks):
+            logits = result.tile([P, U_STEP, VOCAB], F32)
+            for i, v0, acc in banks:
+                nc.vector.tensor_tensor(
+                    out=logits[:, i, v0 : v0 + BANK],
+                    in0=acc[:],
+                    in1=b_out_sb[:, v0 : v0 + BANK],
+                    op=ADD,
                 )
-                nc.sync.dma_start(
-                    out=out_rows[pair * P : (pair + 1) * P, u0 : u0 + U_STEP, :], in_=logits[:]
-                )
+            flat = logits[:].rearrange("p i v -> p (i v)")
+            nc.gpsimd.tensor_scalar(
+                out=flat, in0=flat, scalar1=CLAMP, scalar2=-CLAMP, op0=MIN, op1=MAX
+            )
+            nc.sync.dma_start(
+                out=out_rows[pair * P : (pair + 1) * P, u0 : u0 + U_STEP, :], in_=logits[:]
+            )
+
+        grouped_next = joint_round(*rounds[0])
+        project([enc_jobs[1]])
+        nc.vector.tensor_copy(out=enc_T[1][:], in_=enc_jobs[1]["turned"])
+        banks_before = None
+        for s in range(len(rounds)):
+            grouped_now = grouped_next
+            if s + 1 < len(rounds):
+                grouped_next = joint_round(*rounds[s + 1])
+            banks_now = multiply_round(grouped_now)
+            if s > 0:
+                finish_round(rounds[s - 1][0], rounds[s - 1][1], banks_before)
+            banks_before = banks_now
+        finish_round(rounds[-1][0], rounds[-1][1], banks_before)

@@ -59,8 +59,8 @@ def tile_jointnetwork_kernel(
     with ExitStack() as ctx:
         keep = ctx.enter_context(tc.tile_pool(name="keep", bufs=1))
         stage = ctx.enter_context(tc.tile_pool(name="stage", bufs=3))
-        work = ctx.enter_context(tc.tile_pool(name="work", bufs=3))
-        result = ctx.enter_context(tc.tile_pool(name="result", bufs=4))
+        work = ctx.enter_context(tc.tile_pool(name="work", bufs=4))
+        result = ctx.enter_context(tc.tile_pool(name="result", bufs=6))
         psum = ctx.enter_context(tc.psum_pool(name="psum", bufs=8))
         ctx.enter_context(tc.manual_schedule())
 
@@ -152,24 +152,27 @@ def tile_jointnetwork_kernel(
         rounds = [(pair, u0) for pair in range(BATCH // 2) for u0 in range(0, U_LEN, U_STEP)]
 
         def joint_round(pair, u0):
-            planes = work.tile([P, PACK, U_STEP, P], BF16)
+            planes = []
             for i in range(U_STEP):
+                plane = work.tile([P, PACK, P], BF16, name="plane%d" % i)
+                planes.append(plane)
                 for half in range(2):
                     rows = slice(half * T_LEN, (half + 1) * T_LEN)
                     col = (2 * pair + half) * U_LEN + u0 + i
                     for j in range(PACK):
                         nc.scalar.activation(
-                            out=planes[:, j, i, rows],
+                            out=plane[:, j, rows],
                             in_=enc_T[pair][:, j, rows],
                             func=TANH,
                             bias=pred_T[:, j, col : col + 1],
                             scale=1.0,
                         )
-            grouped = work.tile([P, U_STEP * P, PACK], BF16, align_bytes=64)
-            nc.scalar.copy(
-                out=grouped[:].rearrange("p (c r) j -> p c j r", r=4),
-                in_=planes[:].rearrange("p j i m -> p j (i m)").rearrange("p j (c r) -> p c j r", r=4),
-            )
+            grouped = work.tile([P, U_STEP, P, PACK], BF16, align_bytes=64)
+            for i in range(U_STEP):
+                nc.scalar.copy(
+                    out=grouped[:, i, :, :].rearrange("p (c r) j -> p c j r", r=4),
+                    in_=planes[i][:].rearrange("p j (c r) -> p c j r", r=4),
+                )
             return grouped
 
         def multiply_round(grouped):
@@ -178,7 +181,7 @@ def tile_jointnetwork_kernel(
             nc.vector.quantize_mx(
                 out=codes[:].bitcast(FP8X4),
                 scales=scales[:],
-                in_=grouped[:].rearrange("p c j -> p (c j)"),
+                in_=grouped[:].rearrange("p i c j -> p (i c j)"),
             )
             banks = []
             for i in range(U_STEP):

@@ -25,19 +25,22 @@ U_STEP = 2
 FLOPS = 2 * DEPTH * (BATCH * T_LEN * DEPTH + BATCH * U_LEN * DEPTH + BATCH * T_LEN * U_LEN * VOCAB)
 
 
-def load_weight(nc, keep, words, scales, label):
+def weight_tiles(nc, keep, words, label):
     cols = words.shape[2]
     codes = keep.tile([P, PACK * cols], U8, name=label + "_codes", align_bytes=64)
     scale_rows = keep.tile([P, cols], U8, name=label + "_scales", align_bytes=64)
     nc.vector.memset(scale_rows[:].bitcast(I32), 0)
+    return codes, scale_rows
+
+
+def load_codes(nc, codes, words):
     nc.sync.dma_start(
         out=codes[:].bitcast(I32), in_=words[0].rearrange("p n t -> p (n t)").bitcast(I32)
     )
-    for r in range(4):
-        nc.sync.dma_start(
-            out=scale_rows[r:P:32, :].bitcast(I32), in_=scales[0, r:16:4, :].bitcast(I32)
-        )
-    return codes, scale_rows
+
+
+def load_scale_rows(queue, view, scale_rows, scales, r):
+    queue.dma_start(out=scale_rows[r:P:32, :].bitcast(view), in_=scales[0, r:16:4, :].bitcast(view))
 
 
 def tile_jointnetwork_kernel(
@@ -67,25 +70,37 @@ def tile_jointnetwork_kernel(
         enc_rows = encoder_out.flatten_outer_dims()
         x_pred = keep.tile([P, DEPTH], BF16)
         x_enc = [keep.tile([P, DEPTH], BF16, name="x_enc%d" % pair) for pair in range(2)]
-        nc.scalar.dma_start(out=x_pred[:], in_=predictor_out.flatten_outer_dims())
-        nc.scalar.dma_start(out=x_enc[0][:], in_=enc_rows[0:P, :])
-        w_pred, w_pred_scales = load_weight(nc, keep, W_pred_words, W_pred_scales, "w_pred")
-        w_enc, w_enc_scales = load_weight(nc, keep, W_enc_words, W_enc_scales, "w_enc")
         b_enc_sb = keep.tile([P, PACK], BF16)
         b_pred_sb = keep.tile([P, PACK], BF16)
-        nc.scalar.dma_start(out=b_enc_sb[:], in_=b_enc.rearrange("(p j) -> p j", j=PACK))
-        nc.scalar.dma_start(out=b_pred_sb[:], in_=b_pred.rearrange("(p j) -> p j", j=PACK))
-        nc.scalar.dma_start(out=x_enc[1][:], in_=enc_rows[P : 2 * P, :])
-        w_out, w_out_scales = load_weight(nc, keep, W_out_words, W_out_scales, "w_out")
         b_out_sb = keep.tile([P, VOCAB], BF16)
+        warm = keep.tile([P, 1], F32)
+        nc.vector.memset(warm[:], 0.0)
+        w_pred, w_pred_scales = weight_tiles(nc, keep, W_pred_words, "w_pred")
+        w_enc, w_enc_scales = weight_tiles(nc, keep, W_enc_words, "w_enc")
+        w_out, w_out_scales = weight_tiles(nc, keep, W_out_words, "w_out")
+        nc.scalar.dma_start(out=x_pred[:], in_=predictor_out.flatten_outer_dims())
+        nc.scalar.dma_start(out=x_enc[0][:], in_=enc_rows[0:P, :])
+        load_codes(nc, w_pred, W_pred_words)
+        load_codes(nc, w_enc, W_enc_words)
+        load_scale_rows(nc.sync, I32, w_pred_scales, W_pred_scales, 0)
+        load_scale_rows(nc.sync, I32, w_pred_scales, W_pred_scales, 1)
+        load_scale_rows(nc.scalar, F32, w_pred_scales, W_pred_scales, 2)
+        load_scale_rows(nc.scalar, F32, w_pred_scales, W_pred_scales, 3)
+        nc.scalar.activation(out=warm[:], in_=warm[:], func=TANH)
+        load_scale_rows(nc.sync, I32, w_enc_scales, W_enc_scales, 0)
+        load_scale_rows(nc.sync, I32, w_enc_scales, W_enc_scales, 1)
+        load_scale_rows(nc.scalar, F32, w_enc_scales, W_enc_scales, 2)
+        load_scale_rows(nc.scalar, F32, w_enc_scales, W_enc_scales, 3)
+        nc.gpsimd.dma_start(out=b_enc_sb[:], in_=b_enc.rearrange("(p j) -> p j", j=PACK))
+        nc.gpsimd.dma_start(out=b_pred_sb[:], in_=b_pred.rearrange("(p j) -> p j", j=PACK))
+        load_codes(nc, w_out, W_out_words)
         nc.scalar.dma_start(out=b_out_sb[:], in_=b_out.partition_broadcast(P))
+        nc.scalar.dma_start(out=x_enc[1][:], in_=enc_rows[P : 2 * P, :])
+        for r in range(4):
+            load_scale_rows(nc.sync, I32, w_out_scales, W_out_scales, r)
 
         identity = keep.tile([P, P], F32)
         make_identity(nc, identity[:])
-
-        warm = keep.tile([P, 1], F32)
-        nc.vector.memset(warm[:], 0.0)
-        nc.scalar.activation(out=warm[:], in_=warm[:], func=TANH)
 
         def project(jobs):
             for job in jobs:

@@ -22,6 +22,7 @@ VOCAB = 1024
 BANK = 512
 CLAMP = 15.0
 U_STEP = 2
+EARLY = 256
 FLOPS = 2 * DEPTH * (BATCH * T_LEN * DEPTH + BATCH * U_LEN * DEPTH + BATCH * T_LEN * U_LEN * VOCAB)
 
 
@@ -215,15 +216,19 @@ def tile_jointnetwork_kernel(
                     banks.append((i, v0, acc))
             return banks
 
-        def finish_round(pair, u0, banks):
-            logits = result.tile([P, U_STEP, VOCAB], F32)
-            for i, v0, acc in banks:
-                nc.vector.tensor_tensor(
-                    out=logits[:, i, v0 : v0 + BANK],
-                    in0=acc[:],
-                    in1=b_out_sb[:, v0 : v0 + BANK],
-                    op=ADD,
-                )
+        def fetch(logits, bank, first, stop):
+            i, v0, acc = bank
+            nc.vector.tensor_tensor(
+                out=logits[:, i, v0 + first : v0 + stop],
+                in0=acc[:, first:stop],
+                in1=b_out_sb[:, v0 + first : v0 + stop],
+                op=ADD,
+            )
+
+        def finish_round(pair, u0, banks, logits):
+            fetch(logits, banks[0], EARLY, BANK)
+            for bank in banks[1:]:
+                fetch(logits, bank, 0, BANK)
             flat = logits[:].rearrange("p i v -> p (i v)")
             nc.gpsimd.tensor_scalar(
                 out=flat, in0=flat, scalar1=CLAMP, scalar2=-CLAMP, op0=MIN, op1=MAX
@@ -236,12 +241,15 @@ def tile_jointnetwork_kernel(
         project([enc_jobs[1]])
         nc.vector.tensor_copy(out=enc_T[1][:], in_=enc_jobs[1]["turned"])
         banks_before = None
-        for s in range(len(rounds)):
-            grouped_now = grouped_next
-            if s + 1 < len(rounds):
-                grouped_next = joint_round(*rounds[s + 1])
-            banks_now = multiply_round(grouped_now)
+        for s in range(len(rounds) + 1):
             if s > 0:
-                finish_round(rounds[s - 1][0], rounds[s - 1][1], banks_before)
+                logits = result.tile([P, U_STEP, VOCAB], F32, name="logits")
+                fetch(logits, banks_before[0], 0, EARLY)
+            if s < len(rounds):
+                grouped_now = grouped_next
+                if s + 1 < len(rounds):
+                    grouped_next = joint_round(*rounds[s + 1])
+                banks_now = multiply_round(grouped_now)
+            if s > 0:
+                finish_round(rounds[s - 1][0], rounds[s - 1][1], banks_before, logits)
             banks_before = banks_now
-        finish_round(rounds[-1][0], rounds[-1][1], banks_before)

@@ -13,6 +13,7 @@ TANH = mybir.ActivationFunctionType.Tanh
 ADD = mybir.AluOpType.add
 MIN = mybir.AluOpType.min
 MAX = mybir.AluOpType.max
+MULT = mybir.AluOpType.mult
 
 P = 128
 PACK = 4
@@ -23,6 +24,9 @@ BANK = 512
 CLAMP = 15.0
 U_STEP = 2
 EARLY = 256
+VECTOR_REGROUPS = 1
+GPSIMD_REGROUPS = 2
+VECTOR_CLAMPS = 0
 FLOPS = 2 * DEPTH * (BATCH * T_LEN * DEPTH + BATCH * U_LEN * DEPTH + BATCH * T_LEN * U_LEN * VOCAB)
 
 
@@ -74,6 +78,8 @@ def tile_jointnetwork_kernel(
         b_enc_sb = keep.tile([P, PACK], BF16)
         b_pred_sb = keep.tile([P, PACK], BF16)
         b_out_sb = keep.tile([P, VOCAB], BF16)
+        identity = keep.tile([P, P], F32)
+        make_identity(nc, identity[:])
         warm = keep.tile([P, 1], F32)
         nc.vector.memset(warm[:], 0.0)
         w_pred, w_pred_scales = weight_tiles(nc, keep, W_pred_words, "w_pred")
@@ -100,62 +106,63 @@ def tile_jointnetwork_kernel(
         for r in range(4):
             load_scale_rows(nc.sync, I32, w_out_scales, W_out_scales, r)
 
-        identity = keep.tile([P, P], F32)
-        make_identity(nc, identity[:])
+        def turn_x(job):
+            x_words = job["x"].bitcast(F32)
+            pairs = psum.tile([P, BANK], F32, tag="bank")
+            job["pairs"] = pairs[:, 0 : 2 * P].rearrange("p (h r) -> p h r", h=2)
+            for h in range(2):
+                nc.tensor.transpose(job["pairs"][:, h, :], x_words[:, h : DEPTH // 2 : 2], identity[:])
 
-        def project(jobs):
-            for job in jobs:
-                x_words = job["x"][:].bitcast(F32)
-                pairs = psum.tile([P, BANK], F32, tag="bank")
-                job["pairs"] = pairs[:, 0 : 2 * P].rearrange("p (h r) -> p h r", h=2)
-                for h in range(2):
-                    nc.tensor.transpose(
-                        job["pairs"][:, h, :], x_words[:, h : DEPTH // 2 : 2], identity[:]
-                    )
-            for job in jobs:
-                grouped = stage.tile([P, PACK * P], BF16, align_bytes=64)
-                job["grouped"] = grouped
-                job["copy"](
-                    out=grouped[:].bitcast(F32).rearrange("p (r h) -> p r h", h=2),
-                    in_=job["pairs"].rearrange("p h r -> p r h"),
-                )
-            for job in jobs:
-                x_codes = stage.tile([P, P], U32, align_bytes=64)
-                x_scales = stage.tile([P, P], U8, align_bytes=64)
-                nc.vector.quantize_mx(
-                    out=x_codes[:].bitcast(FP8X4), scales=x_scales[:], in_=job["grouped"][:]
-                )
-                product = psum.tile([P, BANK], F32, tag="bank")
-                job["product"] = product
-                nc.tensor.matmul_mx(
-                    out=product[:],
-                    lhsT=x_codes[:].bitcast(FP8X4),
-                    lhsT_scale=x_scales[:],
-                    rhs=job["w"][:].bitcast(FP8X4),
-                    rhs_scale=job["w_scales"][:],
-                    start=True,
-                    stop=True,
-                )
-            for job in jobs:
-                by_j = stage.tile([P, PACK, P], F32)
-                job["by_j"] = by_j
-                job["copy"](out=by_j[:], in_=job["product"][:].rearrange("r (p j) -> r j p", j=PACK))
-            for job in jobs:
-                turned = psum.tile([P, BANK], F32, tag="bank")
-                job["turned"] = turned[:].rearrange("p (j r) -> p j r", j=PACK)
-                for j in range(PACK):
-                    nc.tensor.transpose(job["turned"][:, j, :], job["by_j"][:, j, :], identity[:])
+        def group_x(job, copy):
+            grouped = stage.tile([P, PACK * P], BF16, align_bytes=64, name="x_grouped")
+            job["grouped"] = grouped
+            copy(
+                out=grouped[:].bitcast(F32).rearrange("p (r h) -> p r h", h=2),
+                in_=job["pairs"].rearrange("p h r -> p r h"),
+            )
+
+        def multiply_x(job):
+            x_codes = stage.tile([P, P], U32, align_bytes=64, name="x_codes")
+            x_scales = stage.tile([P, P], U8, align_bytes=64, name="x_scales")
+            nc.vector.quantize_mx(
+                out=x_codes[:].bitcast(FP8X4), scales=x_scales[:], in_=job["grouped"][:]
+            )
+            product = psum.tile([P, BANK], F32, tag="bank")
+            job["product"] = product
+            nc.tensor.matmul_mx(
+                out=product[:],
+                lhsT=x_codes[:].bitcast(FP8X4),
+                lhsT_scale=x_scales[:],
+                rhs=job["w"][:].bitcast(FP8X4),
+                rhs_scale=job["w_scales"][:],
+                start=True,
+                stop=True,
+            )
+
+        def turn_back(job, copy):
+            by_j = stage.tile([P, PACK, P], F32, name="by_j")
+            copy(out=by_j[:], in_=job["product"][:].rearrange("r (p j) -> r j p", j=PACK))
+            turned = psum.tile([P, BANK], F32, tag="bank")
+            job["turned"] = turned[:].rearrange("p (j r) -> p j r", j=PACK)
+            for j in range(PACK):
+                nc.tensor.transpose(job["turned"][:, j, :], by_j[:, j, :], identity[:])
 
         pred_T = keep.tile([P, PACK, P], F32)
         enc_T = [keep.tile([P, PACK, P], F32, name="enc_T%d" % pair) for pair in range(2)]
-        pred_job = {"x": x_pred, "w": w_pred, "w_scales": w_pred_scales, "copy": nc.vector.tensor_copy}
+        pred_job = {"x": x_pred[:], "w": w_pred, "w_scales": w_pred_scales}
         enc_jobs = [
-            {"x": x_enc[0], "w": w_enc, "w_scales": w_enc_scales, "copy": nc.scalar.copy},
-            {"x": x_enc[1], "w": w_enc, "w_scales": w_enc_scales, "copy": nc.vector.tensor_copy},
+            {"x": x_enc[pair][:], "w": w_enc, "w_scales": w_enc_scales} for pair in range(2)
         ]
-        project([pred_job, enc_jobs[0]])
+        turn_x(pred_job)
+        turn_x(enc_jobs[0])
+        group_x(pred_job, nc.vector.tensor_copy)
+        group_x(enc_jobs[0], nc.scalar.copy)
+        multiply_x(pred_job)
+        multiply_x(enc_jobs[0])
         b_sum = keep.tile([P, PACK], F32)
         nc.vector.tensor_tensor(out=b_sum[:], in0=b_enc_sb[:], in1=b_pred_sb[:], op=ADD)
+        turn_back(pred_job, nc.vector.tensor_copy)
+        turn_back(enc_jobs[0], nc.scalar.copy)
         nc.vector.tensor_tensor(
             out=pred_T[:],
             in0=pred_job["turned"],
@@ -165,11 +172,19 @@ def tile_jointnetwork_kernel(
         nc.scalar.copy(out=enc_T[0][:], in_=enc_jobs[0]["turned"])
 
         out_rows = out.rearrange("b t u v -> (b t) u v")
-        rounds = [(pair, u0) for pair in range(BATCH // 2) for u0 in range(0, U_LEN, U_STEP)]
+        full = [U_STEP] * (U_LEN // U_STEP)
+        rounds = []
+        for pair, pair_widths in ((0, full), (1, full)):
+            u0 = 0
+            for width in pair_widths:
+                rounds.append((pair, u0, width))
+                u0 += width
+        last = len(rounds) - 1
 
-        def joint_round(pair, u0):
+        def tanh_round(s):
+            pair, u0, width = rounds[s]
             planes = []
-            for i in range(U_STEP):
+            for i in range(width):
                 plane = work.tile([P, PACK, P], BF16, name="plane%d" % i)
                 planes.append(plane)
                 for half in range(2):
@@ -183,24 +198,33 @@ def tile_jointnetwork_kernel(
                             bias=pred_T[:, j, col : col + 1],
                             scale=1.0,
                         )
-            grouped = work.tile([P, U_STEP, P, PACK], BF16, align_bytes=64)
-            for i in range(U_STEP):
-                nc.scalar.copy(
-                    out=grouped[:, i, :, :].rearrange("p (c r) j -> p c j r", r=4),
-                    in_=planes[i][:].rearrange("p j (c r) -> p c j r", r=4),
-                )
+            return planes
+
+        def regroup_round(s, planes):
+            width = rounds[s][2]
+            grouped = work.tile([P, U_STEP, P, PACK], BF16, align_bytes=64, name="grouped")
+            for i in range(width):
+                target = grouped[:, i, :, :].rearrange("p (c r) j -> p c j r", r=4)
+                source = planes[i][:].rearrange("p j (c r) -> p c j r", r=4)
+                if s < VECTOR_REGROUPS:
+                    nc.vector.tensor_copy(out=target, in_=source)
+                elif s < VECTOR_REGROUPS + GPSIMD_REGROUPS:
+                    nc.gpsimd.tensor_scalar(out=target, in0=source, scalar1=1.0, scalar2=0.0, op0=MULT, op1=ADD)
+                else:
+                    nc.scalar.copy(out=target, in_=source)
             return grouped
 
-        def multiply_round(grouped):
-            codes = work.tile([P, U_STEP * P], U32, align_bytes=64)
-            scales = work.tile([P, U_STEP * P], U8, align_bytes=64)
+        def multiply_round(s, grouped):
+            width = rounds[s][2]
+            codes = work.tile([P, U_STEP * P], U32, align_bytes=64, name="codes")
+            scales = work.tile([P, U_STEP * P], U8, align_bytes=64, name="scales")
             nc.vector.quantize_mx(
-                out=codes[:].bitcast(FP8X4),
-                scales=scales[:],
-                in_=grouped[:].rearrange("p i c j -> p (i c j)"),
+                out=codes[:, 0 : width * P].bitcast(FP8X4),
+                scales=scales[:, 0 : width * P],
+                in_=grouped[:, 0:width, :, :].rearrange("p i c j -> p (i c j)"),
             )
             banks = []
-            for i in range(U_STEP):
+            for i in range(width):
                 m_cols = slice(i * P, (i + 1) * P)
                 for v0 in range(0, VOCAB, BANK):
                     acc = psum.tile([P, BANK], F32, tag="bank")
@@ -225,31 +249,53 @@ def tile_jointnetwork_kernel(
                 op=ADD,
             )
 
-        def finish_round(pair, u0, banks, logits):
+        def start_round(banks):
+            logits = result.tile([P, U_STEP, VOCAB], F32, name="logits")
+            fetch(logits, banks[0], 0, EARLY)
+            return logits
+
+        def finish_round(banks, logits):
             fetch(logits, banks[0], EARLY, BANK)
             for bank in banks[1:]:
                 fetch(logits, bank, 0, BANK)
-            flat = logits[:].rearrange("p i v -> p (i v)")
-            nc.gpsimd.tensor_scalar(
-                out=flat, in0=flat, scalar1=CLAMP, scalar2=-CLAMP, op0=MIN, op1=MAX
-            )
+
+        def send_round(s, logits):
+            pair, u0, width = rounds[s]
+            engine = nc.vector if s > last - VECTOR_CLAMPS else nc.gpsimd
+            flat = logits[:, 0:width, :].rearrange("p i v -> p (i v)")
+            engine.tensor_scalar(out=flat, in0=flat, scalar1=CLAMP, scalar2=-CLAMP, op0=MIN, op1=MAX)
             nc.sync.dma_start(
-                out=out_rows[pair * P : (pair + 1) * P, u0 : u0 + U_STEP, :], in_=logits[:]
+                out=out_rows[pair * P : (pair + 1) * P, u0 : u0 + width, :], in_=logits[:, 0:width, :]
             )
 
-        grouped_next = joint_round(*rounds[0])
-        project([enc_jobs[1]])
-        nc.vector.tensor_copy(out=enc_T[1][:], in_=enc_jobs[1]["turned"])
+        planes_next = tanh_round(0)
+        turn_x(enc_jobs[1])
+        group_x(enc_jobs[1], nc.vector.tensor_copy)
+        multiply_x(enc_jobs[1])
+        turn_back(enc_jobs[1], nc.vector.tensor_copy)
+        grouped_next = regroup_round(0, planes_next)
         banks_before = None
+        held = []
         for s in range(len(rounds) + 1):
             if s > 0:
-                logits = result.tile([P, U_STEP, VOCAB], F32, name="logits")
-                fetch(logits, banks_before[0], 0, EARLY)
+                logits = start_round(banks_before)
             if s < len(rounds):
                 grouped_now = grouped_next
                 if s + 1 < len(rounds):
-                    grouped_next = joint_round(*rounds[s + 1])
-                banks_now = multiply_round(grouped_now)
+                    planes_next = tanh_round(s + 1)
+                    if s + 1 >= VECTOR_REGROUPS:
+                        grouped_next = regroup_round(s + 1, planes_next)
+                banks_now = multiply_round(s, grouped_now)
+                if s == 0:
+                    nc.vector.tensor_copy(out=enc_T[1][:], in_=enc_jobs[1]["turned"])
+                if s + 1 < VECTOR_REGROUPS:
+                    grouped_next = regroup_round(s + 1, planes_next)
             if s > 0:
-                finish_round(rounds[s - 1][0], rounds[s - 1][1], banks_before, logits)
+                finish_round(banks_before, logits)
+                if s - 1 > last - VECTOR_CLAMPS:
+                    held.append((s - 1, logits))
+                else:
+                    send_round(s - 1, logits)
             banks_before = banks_now
+        for s, logits in held:
+            send_round(s, logits)

@@ -23,10 +23,9 @@ VOCAB = 1024
 BANK = 512
 CLAMP = 15.0
 U_STEP = 2
-EARLY = 256
 VECTOR_REGROUPS = 1
 GPSIMD_REGROUPS = 2
-VECTOR_CLAMPS = 0
+SPLIT_ROUNDS = 2
 FLOPS = 2 * DEPTH * (BATCH * T_LEN * DEPTH + BATCH * U_LEN * DEPTH + BATCH * T_LEN * U_LEN * VOCAB)
 
 
@@ -240,62 +239,42 @@ def tile_jointnetwork_kernel(
                     banks.append((i, v0, acc))
             return banks
 
-        def fetch(logits, bank, first, stop):
-            i, v0, acc = bank
-            nc.vector.tensor_tensor(
-                out=logits[:, i, v0 + first : v0 + stop],
-                in0=acc[:, first:stop],
-                in1=b_out_sb[:, v0 + first : v0 + stop],
-                op=ADD,
-            )
-
-        def start_round(banks):
-            logits = result.tile([P, U_STEP, VOCAB], F32, name="logits")
-            fetch(logits, banks[0], 0, EARLY)
-            return logits
-
-        def finish_round(banks, logits):
-            fetch(logits, banks[0], EARLY, BANK)
-            for bank in banks[1:]:
-                fetch(logits, bank, 0, BANK)
-
-        def send_round(s, logits):
+        def finish_round(s, banks):
             pair, u0, width = rounds[s]
-            engine = nc.vector if s > last - VECTOR_CLAMPS else nc.gpsimd
-            flat = logits[:, 0:width, :].rearrange("p i v -> p (i v)")
-            engine.tensor_scalar(out=flat, in0=flat, scalar1=CLAMP, scalar2=-CLAMP, op0=MIN, op1=MAX)
-            nc.sync.dma_start(
-                out=out_rows[pair * P : (pair + 1) * P, u0 : u0 + width, :], in_=logits[:, 0:width, :]
-            )
+            rows_out = out_rows[pair * P : (pair + 1) * P, :, :]
+            logits = result.tile([P, U_STEP, VOCAB], F32, name="logits")
+            for i, v0, acc in banks:
+                nc.vector.tensor_tensor(
+                    out=logits[:, i, v0 : v0 + BANK],
+                    in0=acc[:],
+                    in1=b_out_sb[:, v0 : v0 + BANK],
+                    op=ADD,
+                )
+                if s > last - SPLIT_ROUNDS and v0 + BANK == VOCAB:
+                    engine = nc.vector if (s == last and i == width - 1) else nc.gpsimd
+                    engine.tensor_scalar(
+                        out=logits[:, i, :], in0=logits[:, i, :], scalar1=CLAMP, scalar2=-CLAMP, op0=MIN, op1=MAX
+                    )
+                    nc.sync.dma_start(out=rows_out[:, u0 + i, :], in_=logits[:, i, :])
+            if s > last - SPLIT_ROUNDS:
+                return
+            flat = logits[:].rearrange("p i v -> p (i v)")
+            nc.gpsimd.tensor_scalar(out=flat, in0=flat, scalar1=CLAMP, scalar2=-CLAMP, op0=MIN, op1=MAX)
+            nc.sync.dma_start(out=rows_out[:, u0 : u0 + width, :], in_=logits[:])
 
-        planes_next = tanh_round(0)
+        planes = tanh_round(0)
         turn_x(enc_jobs[1])
         group_x(enc_jobs[1], nc.vector.tensor_copy)
         multiply_x(enc_jobs[1])
         turn_back(enc_jobs[1], nc.vector.tensor_copy)
-        grouped_next = regroup_round(0, planes_next)
-        banks_before = None
-        held = []
-        for s in range(len(rounds) + 1):
-            if s > 0:
-                logits = start_round(banks_before)
-            if s < len(rounds):
-                grouped_now = grouped_next
-                if s + 1 < len(rounds):
-                    planes_next = tanh_round(s + 1)
-                    if s + 1 >= VECTOR_REGROUPS:
-                        grouped_next = regroup_round(s + 1, planes_next)
-                banks_now = multiply_round(s, grouped_now)
-                if s == 0:
-                    nc.vector.tensor_copy(out=enc_T[1][:], in_=enc_jobs[1]["turned"])
-                if s + 1 < VECTOR_REGROUPS:
-                    grouped_next = regroup_round(s + 1, planes_next)
-            if s > 0:
-                finish_round(banks_before, logits)
-                if s - 1 > last - VECTOR_CLAMPS:
-                    held.append((s - 1, logits))
-                else:
-                    send_round(s - 1, logits)
-            banks_before = banks_now
-        for s, logits in held:
-            send_round(s, logits)
+        banks = {0: multiply_round(0, regroup_round(0, planes))}
+        nc.vector.tensor_copy(out=enc_T[1][:], in_=enc_jobs[1]["turned"])
+        grouped = {s: regroup_round(s, tanh_round(s)) for s in (1, 2)}
+        finish_round(0, banks[0])
+        banks[1] = multiply_round(1, grouped[1])
+        for s in range(1, len(rounds)):
+            if s + 2 < len(rounds):
+                grouped[s + 2] = regroup_round(s + 2, tanh_round(s + 2))
+            if s + 1 < len(rounds):
+                banks[s + 1] = multiply_round(s + 1, grouped[s + 1])
+            finish_round(s, banks[s])

@@ -23,8 +23,8 @@ VOCAB = 1024
 BANK = 512
 CLAMP = 15.0
 U_STEP = 2
-VECTOR_REGROUPS = 1
-GPSIMD_REGROUPS = 2
+VECTOR_REGROUPS = 2
+GPSIMD_REGROUPS = 0
 SPLIT_ROUNDS = 2
 FLOPS = 2 * DEPTH * (BATCH * T_LEN * DEPTH + BATCH * U_LEN * DEPTH + BATCH * T_LEN * U_LEN * VOCAB)
 
@@ -87,21 +87,20 @@ def tile_jointnetwork_kernel(
         nc.scalar.dma_start(out=x_pred[:], in_=predictor_out.flatten_outer_dims())
         nc.scalar.dma_start(out=x_enc[0][:], in_=enc_rows[0:P, :])
         load_codes(nc, w_pred, W_pred_words)
-        load_codes(nc, w_enc, W_enc_words)
         load_scale_rows(nc.sync, I32, w_pred_scales, W_pred_scales, 0)
         load_scale_rows(nc.sync, I32, w_pred_scales, W_pred_scales, 1)
         load_scale_rows(nc.scalar, F32, w_pred_scales, W_pred_scales, 2)
         load_scale_rows(nc.scalar, F32, w_pred_scales, W_pred_scales, 3)
+        load_codes(nc, w_enc, W_enc_words)
         nc.scalar.activation(out=warm[:], in_=warm[:], func=TANH)
         load_scale_rows(nc.sync, I32, w_enc_scales, W_enc_scales, 0)
         load_scale_rows(nc.sync, I32, w_enc_scales, W_enc_scales, 1)
         load_scale_rows(nc.scalar, F32, w_enc_scales, W_enc_scales, 2)
         load_scale_rows(nc.scalar, F32, w_enc_scales, W_enc_scales, 3)
-        nc.gpsimd.dma_start(out=b_enc_sb[:], in_=b_enc.rearrange("(p j) -> p j", j=PACK))
-        nc.gpsimd.dma_start(out=b_pred_sb[:], in_=b_pred.rearrange("(p j) -> p j", j=PACK))
+        nc.sync.dma_start(out=b_enc_sb[:], in_=b_enc.rearrange("(p j) -> p j", j=PACK))
+        nc.sync.dma_start(out=b_pred_sb[:], in_=b_pred.rearrange("(p j) -> p j", j=PACK))
+        nc.gpsimd.dma_start(out=x_enc[1][:], in_=enc_rows[P : 2 * P, :])
         load_codes(nc, w_out, W_out_words)
-        nc.scalar.dma_start(out=b_out_sb[:], in_=b_out.partition_broadcast(P))
-        nc.scalar.dma_start(out=x_enc[1][:], in_=enc_rows[P : 2 * P, :])
         for r in range(4):
             load_scale_rows(nc.sync, I32, w_out_scales, W_out_scales, r)
 
@@ -158,10 +157,11 @@ def tile_jointnetwork_kernel(
         group_x(enc_jobs[0], nc.scalar.copy)
         multiply_x(pred_job)
         multiply_x(enc_jobs[0])
-        b_sum = keep.tile([P, PACK], F32)
-        nc.vector.tensor_tensor(out=b_sum[:], in0=b_enc_sb[:], in1=b_pred_sb[:], op=ADD)
         turn_back(pred_job, nc.vector.tensor_copy)
         turn_back(enc_jobs[0], nc.scalar.copy)
+        nc.scalar.dma_start(out=b_out_sb[:], in_=b_out.partition_broadcast(P))
+        b_sum = keep.tile([P, PACK], F32)
+        nc.vector.tensor_tensor(out=b_sum[:], in0=b_enc_sb[:], in1=b_pred_sb[:], op=ADD)
         nc.vector.tensor_tensor(
             out=pred_T[:],
             in0=pred_job["turned"],
@@ -262,19 +262,23 @@ def tile_jointnetwork_kernel(
             nc.gpsimd.tensor_scalar(out=flat, in0=flat, scalar1=CLAMP, scalar2=-CLAMP, op0=MIN, op1=MAX)
             nc.sync.dma_start(out=rows_out[:, u0 : u0 + width, :], in_=logits[:])
 
-        planes = tanh_round(0)
+        planes = {0: tanh_round(0)}
         turn_x(enc_jobs[1])
         group_x(enc_jobs[1], nc.vector.tensor_copy)
         multiply_x(enc_jobs[1])
         turn_back(enc_jobs[1], nc.vector.tensor_copy)
-        banks = {0: multiply_round(0, regroup_round(0, planes))}
-        nc.vector.tensor_copy(out=enc_T[1][:], in_=enc_jobs[1]["turned"])
-        grouped = {s: regroup_round(s, tanh_round(s)) for s in (1, 2)}
-        finish_round(0, banks[0])
-        banks[1] = multiply_round(1, grouped[1])
-        for s in range(1, len(rounds)):
-            if s + 2 < len(rounds):
-                grouped[s + 2] = regroup_round(s + 2, tanh_round(s + 2))
+        grouped = {0: regroup_round(0, planes[0])}
+        banks = {}
+        for s in range(len(rounds) + 1):
             if s + 1 < len(rounds):
-                banks[s + 1] = multiply_round(s + 1, grouped[s + 1])
-            finish_round(s, banks[s])
+                planes[s + 1] = tanh_round(s + 1)
+                if s + 1 >= VECTOR_REGROUPS:
+                    grouped[s + 1] = regroup_round(s + 1, planes[s + 1])
+            if s < len(rounds):
+                banks[s] = multiply_round(s, grouped[s])
+            if s == 0:
+                nc.vector.tensor_copy(out=enc_T[1][:], in_=enc_jobs[1]["turned"])
+            if s + 1 < VECTOR_REGROUPS:
+                grouped[s + 1] = regroup_round(s + 1, planes[s + 1])
+            if s > 0:
+                finish_round(s - 1, banks[s - 1])

@@ -159,7 +159,6 @@ def tile_jointnetwork_kernel(
         multiply_x(enc_jobs[0])
         turn_back(pred_job, nc.vector.tensor_copy)
         turn_back(enc_jobs[0], nc.scalar.copy)
-        nc.scalar.dma_start(out=b_out_sb[:], in_=b_out.partition_broadcast(P))
         b_sum = keep.tile([P, PACK], F32)
         nc.vector.tensor_tensor(out=b_sum[:], in0=b_enc_sb[:], in1=b_pred_sb[:], op=ADD)
         nc.vector.tensor_tensor(
@@ -169,6 +168,7 @@ def tile_jointnetwork_kernel(
             op=ADD,
         )
         nc.scalar.copy(out=enc_T[0][:], in_=enc_jobs[0]["turned"])
+        nc.scalar.dma_start(out=b_out_sb[:], in_=b_out.partition_broadcast(P))
 
         out_rows = out.rearrange("b t u v -> (b t) u v")
         full = [U_STEP] * (U_LEN // U_STEP)

from contextlib import ExitStack

import concourse.mybir as mybir
from concourse.masks import make_identity

F32 = mybir.dt.float32
BF16 = mybir.dt.bfloat16
I32 = mybir.dt.int32
U32 = mybir.dt.uint32
U8 = mybir.dt.uint8
FP8X4 = mybir.dt.float8_e4m3fn_x4
TANH = mybir.ActivationFunctionType.Tanh
ADD = mybir.AluOpType.add
MIN = mybir.AluOpType.min
MAX = mybir.AluOpType.max
MULT = mybir.AluOpType.mult

P = 128
PACK = 4
BATCH, T_LEN, U_LEN = 4, 64, 32
DEPTH = P * PACK
VOCAB = 1024
BANK = 512
CLAMP = 15.0
U_STEP = 2
VECTOR_REGROUPS = 2
GPSIMD_REGROUPS = 0
SPLIT_ROUNDS = 2
FLOPS = 2 * DEPTH * (BATCH * T_LEN * DEPTH + BATCH * U_LEN * DEPTH + BATCH * T_LEN * U_LEN * VOCAB)


def weight_tiles(nc, keep, words, label):
    cols = words.shape[2]
    codes = keep.tile([P, PACK * cols], U8, name=label + "_codes", align_bytes=64)
    scale_rows = keep.tile([P, cols], U8, name=label + "_scales", align_bytes=64)
    nc.vector.memset(scale_rows[:].bitcast(I32), 0)
    return codes, scale_rows


def load_codes(nc, codes, words):
    nc.sync.dma_start(
        out=codes[:].bitcast(I32), in_=words[0].rearrange("p n t -> p (n t)").bitcast(I32)
    )


def load_scale_rows(queue, view, scale_rows, scales, r):
    queue.dma_start(out=scale_rows[r:P:32, :].bitcast(view), in_=scales[0, r:16:4, :].bitcast(view))


def tile_jointnetwork_kernel(
    tc,
    encoder_out,
    predictor_out,
    W_enc_words,
    W_enc_scales,
    b_enc,
    W_pred_words,
    W_pred_scales,
    b_pred,
    W_out_words,
    W_out_scales,
    b_out,
    out,
):
    nc = tc.nc
    with ExitStack() as ctx:
        keep = ctx.enter_context(tc.tile_pool(name="keep", bufs=1))
        stage = ctx.enter_context(tc.tile_pool(name="stage", bufs=3))
        work = ctx.enter_context(tc.tile_pool(name="work", bufs=4))
        result = ctx.enter_context(tc.tile_pool(name="result", bufs=6))
        psum = ctx.enter_context(tc.psum_pool(name="psum", bufs=8))
        ctx.enter_context(tc.manual_schedule())

        enc_rows = encoder_out.flatten_outer_dims()
        x_pred = keep.tile([P, DEPTH], BF16)
        x_enc = [keep.tile([P, DEPTH], BF16, name="x_enc%d" % pair) for pair in range(2)]
        b_enc_sb = keep.tile([P, PACK], BF16)
        b_pred_sb = keep.tile([P, PACK], BF16)
        b_out_sb = keep.tile([P, VOCAB], BF16)
        identity = keep.tile([P, P], F32)
        make_identity(nc, identity[:])
        warm = keep.tile([P, 1], F32)
        nc.vector.memset(warm[:], 0.0)
        w_pred, w_pred_scales = weight_tiles(nc, keep, W_pred_words, "w_pred")
        w_enc, w_enc_scales = weight_tiles(nc, keep, W_enc_words, "w_enc")
        w_out, w_out_scales = weight_tiles(nc, keep, W_out_words, "w_out")
        nc.scalar.dma_start(out=x_pred[:], in_=predictor_out.flatten_outer_dims())
        nc.scalar.dma_start(out=x_enc[0][:], in_=enc_rows[0:P, :])
        load_codes(nc, w_pred, W_pred_words)
        load_scale_rows(nc.sync, I32, w_pred_scales, W_pred_scales, 0)
        load_scale_rows(nc.sync, I32, w_pred_scales, W_pred_scales, 1)
        load_scale_rows(nc.scalar, F32, w_pred_scales, W_pred_scales, 2)
        load_scale_rows(nc.scalar, F32, w_pred_scales, W_pred_scales, 3)
        load_codes(nc, w_enc, W_enc_words)
        nc.scalar.activation(out=warm[:], in_=warm[:], func=TANH)
        load_scale_rows(nc.sync, I32, w_enc_scales, W_enc_scales, 0)
        load_scale_rows(nc.sync, I32, w_enc_scales, W_enc_scales, 1)
        load_scale_rows(nc.scalar, F32, w_enc_scales, W_enc_scales, 2)
        load_scale_rows(nc.scalar, F32, w_enc_scales, W_enc_scales, 3)
        nc.sync.dma_start(out=b_enc_sb[:], in_=b_enc.rearrange("(p j) -> p j", j=PACK))
        nc.sync.dma_start(out=b_pred_sb[:], in_=b_pred.rearrange("(p j) -> p j", j=PACK))
        nc.gpsimd.dma_start(out=x_enc[1][:], in_=enc_rows[P : 2 * P, :])
        load_codes(nc, w_out, W_out_words)
        for r in range(4):
            load_scale_rows(nc.sync, I32, w_out_scales, W_out_scales, r)

        def turn_x(job):
            x_words = job["x"].bitcast(F32)
            pairs = psum.tile([P, BANK], F32, tag="bank")
            job["pairs"] = pairs[:, 0 : 2 * P].rearrange("p (h r) -> p h r", h=2)
            for h in range(2):
                nc.tensor.transpose(job["pairs"][:, h, :], x_words[:, h : DEPTH // 2 : 2], identity[:])

        def group_x(job, copy):
            grouped = stage.tile([P, PACK * P], BF16, align_bytes=64, name="x_grouped")
            job["grouped"] = grouped
            copy(
                out=grouped[:].bitcast(F32).rearrange("p (r h) -> p r h", h=2),
                in_=job["pairs"].rearrange("p h r -> p r h"),
            )

        def multiply_x(job):
            x_codes = stage.tile([P, P], U32, align_bytes=64, name="x_codes")
            x_scales = stage.tile([P, P], U8, align_bytes=64, name="x_scales")
            nc.vector.quantize_mx(
                out=x_codes[:].bitcast(FP8X4), scales=x_scales[:], in_=job["grouped"][:]
            )
            product = psum.tile([P, BANK], F32, tag="bank")
            job["product"] = product
            nc.tensor.matmul_mx(
                out=product[:],
                lhsT=x_codes[:].bitcast(FP8X4),
                lhsT_scale=x_scales[:],
                rhs=job["w"][:].bitcast(FP8X4),
                rhs_scale=job["w_scales"][:],
                start=True,
                stop=True,
            )

        def turn_back(job, copy):
            by_j = stage.tile([P, PACK, P], F32, name="by_j")
            copy(out=by_j[:], in_=job["product"][:].rearrange("r (p j) -> r j p", j=PACK))
            turned = psum.tile([P, BANK], F32, tag="bank")
            job["turned"] = turned[:].rearrange("p (j r) -> p j r", j=PACK)
            for j in range(PACK):
                nc.tensor.transpose(job["turned"][:, j, :], by_j[:, j, :], identity[:])

        pred_T = keep.tile([P, PACK, P], F32)
        enc_T = [keep.tile([P, PACK, P], F32, name="enc_T%d" % pair) for pair in range(2)]
        pred_job = {"x": x_pred[:], "w": w_pred, "w_scales": w_pred_scales}
        enc_jobs = [
            {"x": x_enc[pair][:], "w": w_enc, "w_scales": w_enc_scales} for pair in range(2)
        ]
        turn_x(pred_job)
        turn_x(enc_jobs[0])
        group_x(pred_job, nc.vector.tensor_copy)
        group_x(enc_jobs[0], nc.scalar.copy)
        multiply_x(pred_job)
        multiply_x(enc_jobs[0])
        turn_back(pred_job, nc.vector.tensor_copy)
        turn_back(enc_jobs[0], nc.scalar.copy)
        b_sum = keep.tile([P, PACK], F32)
        nc.vector.tensor_tensor(out=b_sum[:], in0=b_enc_sb[:], in1=b_pred_sb[:], op=ADD)
        nc.vector.tensor_tensor(
            out=pred_T[:],
            in0=pred_job["turned"],
            in1=b_sum[:].unsqueeze(2).to_broadcast([P, PACK, P]),
            op=ADD,
        )
        nc.scalar.copy(out=enc_T[0][:], in_=enc_jobs[0]["turned"])
        nc.scalar.dma_start(out=b_out_sb[:], in_=b_out.partition_broadcast(P))

        out_rows = out.rearrange("b t u v -> (b t) u v")
        full = [U_STEP] * (U_LEN // U_STEP)
        rounds = []
        for pair, pair_widths in ((0, full), (1, full)):
            u0 = 0
            for width in pair_widths:
                rounds.append((pair, u0, width))
                u0 += width
        last = len(rounds) - 1

        def tanh_round(s):
            pair, u0, width = rounds[s]
            planes = []
            for i in range(width):
                plane = work.tile([P, PACK, P], BF16, name="plane%d" % i)
                planes.append(plane)
                for half in range(2):
                    rows = slice(half * T_LEN, (half + 1) * T_LEN)
                    col = (2 * pair + half) * U_LEN + u0 + i
                    for j in range(PACK):
                        nc.scalar.activation(
                            out=plane[:, j, rows],
                            in_=enc_T[pair][:, j, rows],
                            func=TANH,
                            bias=pred_T[:, j, col : col + 1],
                            scale=1.0,
                        )
            return planes

        def regroup_round(s, planes):
            width = rounds[s][2]
            grouped = work.tile([P, U_STEP, P, PACK], BF16, align_bytes=64, name="grouped")
            for i in range(width):
                target = grouped[:, i, :, :].rearrange("p (c r) j -> p c j r", r=4)
                source = planes[i][:].rearrange("p j (c r) -> p c j r", r=4)
                if s < VECTOR_REGROUPS:
                    nc.vector.tensor_copy(out=target, in_=source)
                elif s < VECTOR_REGROUPS + GPSIMD_REGROUPS:
                    nc.gpsimd.tensor_scalar(out=target, in0=source, scalar1=1.0, scalar2=0.0, op0=MULT, op1=ADD)
                else:
                    nc.scalar.copy(out=target, in_=source)
            return grouped

        def multiply_round(s, grouped):
            width = rounds[s][2]
            codes = work.tile([P, U_STEP * P], U32, align_bytes=64, name="codes")
            scales = work.tile([P, U_STEP * P], U8, align_bytes=64, name="scales")
            nc.vector.quantize_mx(
                out=codes[:, 0 : width * P].bitcast(FP8X4),
                scales=scales[:, 0 : width * P],
                in_=grouped[:, 0:width, :, :].rearrange("p i c j -> p (i c j)"),
            )
            banks = []
            for i in range(width):
                m_cols = slice(i * P, (i + 1) * P)
                for v0 in range(0, VOCAB, BANK):
                    acc = psum.tile([P, BANK], F32, tag="bank")
                    nc.tensor.matmul_mx(
                        out=acc[:],
                        lhsT=codes[:, m_cols].bitcast(FP8X4),
                        lhsT_scale=scales[:, m_cols],
                        rhs=w_out[:, PACK * v0 : PACK * (v0 + BANK)].bitcast(FP8X4),
                        rhs_scale=w_out_scales[:, v0 : v0 + BANK],
                        start=True,
                        stop=True,
                    )
                    banks.append((i, v0, acc))
            return banks

        def finish_round(s, banks):
            pair, u0, width = rounds[s]
            rows_out = out_rows[pair * P : (pair + 1) * P, :, :]
            logits = result.tile([P, U_STEP, VOCAB], F32, name="logits")
            for i, v0, acc in banks:
                nc.vector.tensor_tensor(
                    out=logits[:, i, v0 : v0 + BANK],
                    in0=acc[:],
                    in1=b_out_sb[:, v0 : v0 + BANK],
                    op=ADD,
                )
                if s > last - SPLIT_ROUNDS and v0 + BANK == VOCAB:
                    engine = nc.vector if (s == last and i == width - 1) else nc.gpsimd
                    engine.tensor_scalar(
                        out=logits[:, i, :], in0=logits[:, i, :], scalar1=CLAMP, scalar2=-CLAMP, op0=MIN, op1=MAX
                    )
                    nc.sync.dma_start(out=rows_out[:, u0 + i, :], in_=logits[:, i, :])
            if s > last - SPLIT_ROUNDS:
                return
            flat = logits[:].rearrange("p i v -> p (i v)")
            nc.gpsimd.tensor_scalar(out=flat, in0=flat, scalar1=CLAMP, scalar2=-CLAMP, op0=MIN, op1=MAX)
            nc.sync.dma_start(out=rows_out[:, u0 : u0 + width, :], in_=logits[:])

        planes = {0: tanh_round(0)}
        turn_x(enc_jobs[1])
        group_x(enc_jobs[1], nc.vector.tensor_copy)
        multiply_x(enc_jobs[1])
        turn_back(enc_jobs[1], nc.vector.tensor_copy)
        grouped = {0: regroup_round(0, planes[0])}
        banks = {}
        for s in range(len(rounds) + 1):
            if s + 1 < len(rounds):
                planes[s + 1] = tanh_round(s + 1)
                if s + 1 >= VECTOR_REGROUPS:
                    grouped[s + 1] = regroup_round(s + 1, planes[s + 1])
            if s < len(rounds):
                banks[s] = multiply_round(s, grouped[s])
            if s == 0:
                nc.vector.tensor_copy(out=enc_T[1][:], in_=enc_jobs[1]["turned"])
            if s + 1 < VECTOR_REGROUPS:
                grouped[s + 1] = regroup_round(s + 1, planes[s + 1])
            if s > 0:
                finish_round(s - 1, banks[s - 1])
